import numpy as np
import ml_dtypes


def mxq(x, axis, fmt="e4m3"):
    dtype, down = {"e4m3": (ml_dtypes.float8_e4m3fn, 7), "e5m2": (ml_dtypes.float8_e5m2, 14)}[fmt]
    v = np.moveaxis(np.asarray(x, np.float32).astype(ml_dtypes.bfloat16).astype(np.float64), axis, -1)
    blocks = v.reshape(v.shape[:-1] + (-1, 32))
    amax = np.abs(blocks).max(-1, keepdims=True)
    byte = np.maximum(np.where(amax > 0, np.frexp(amax)[1] - 1 + 127, 0) - down, 1)
    scale = np.exp2(byte - 127.0)
    codes = (blocks / scale).astype(np.float32).astype(dtype).astype(np.float64)
    return np.moveaxis((codes * scale).reshape(v.shape), -1, axis)


WIDE = False


def mx_kscale(k):
    if not WIDE:
        return np.ones(k)
    levels = np.array([10, -10, 5, -5, 0])
    a = np.random.permutation(np.resize(levels, k // 512 * 4)).reshape(k // 512, 4)
    idx = np.arange(k)
    return np.exp2(a[idx // 512, idx % 128 // 32])


BF16 = ml_dtypes.bfloat16


def bf(x):
    return np.asarray(x, np.float32).astype(BF16)


def f64(x):
    return np.asarray(x).astype(np.float64)


E2M1 = np.array([0.0, 0.5, 1.0, 1.5, 2.0, 3.0, 4.0, 6.0, -0.0, -0.5, -1.0, -1.5, -2.0, -3.0, -4.0, -6.0])


def pack_weight(w, fmt):
    k, n = w.shape
    w = f64(bf(w)).reshape(k // 32, 32, n)
    amax = np.abs(w).max(1)
    if fmt == "e4m3":
        byte = np.frexp(amax)[1] - 1 + 127 - 7
    else:
        mant, ex = np.frexp(amax / 6.0)
        byte = np.where(mant > 0.5, ex, ex - 1) + 127
    byte = np.clip(np.where(amax > 0, byte, 1), 1, 254)
    scaled = (w * np.exp2(127.0 - byte)[:, None, :]).reshape(k, n).astype(np.float32)
    by_word = np.ascontiguousarray(scaled.reshape(k // 512, 128, 4, n).transpose(0, 1, 3, 2))
    if fmt == "e4m3":
        words = by_word.astype(ml_dtypes.float8_e4m3fn).view(np.uint8)
    else:
        c = by_word.astype(ml_dtypes.float4_e2m1fn).view(np.uint8) & 0xF
        words = c[..., 0::2] | (c[..., 1::2] << 4)
    return np.ascontiguousarray(words), np.ascontiguousarray(byte.astype(np.uint8).reshape(k // 512, 16, n))


def unpack_weight(words, scales, fmt):
    g, p, n, _ = words.shape
    if fmt == "e4m3":
        vals = np.ascontiguousarray(words).view(ml_dtypes.float8_e4m3fn).astype(np.float64)
    else:
        nib = np.empty((g, p, n, 4), np.uint8)
        nib[..., 0::2] = words & 0xF
        nib[..., 1::2] = words >> 4
        vals = E2M1[nib]
    vals = vals * np.repeat(np.exp2(scales.astype(np.float64) - 127.0), 8, axis=1)[..., None]
    return vals.transpose(0, 1, 3, 2).reshape(g * 512, n)


B, S, E, H, KD, HD, C = 1, 256, 1024, 8, 128, 1024, 512
V = H * HD
EPS = 1e-5
FMT = "e4m3"


def silu(v):
    return v / (1.0 + np.exp(-v))


def setup_inputs():
    s = mx_kscale(E)
    lvl = np.exp2(np.random.uniform(-9.0, 2.0, (B, S, H, 1)))
    x = bf(np.random.standard_normal((B, S, E)) * s)
    wg_words, wg_scales = pack_weight(np.random.standard_normal((E, V)) / np.sqrt(E) / s[:, None], FMT)
    ret = bf(np.random.standard_normal((B, S, H, HD)) * lvl)
    wo_words, wo_scales = pack_weight(np.random.standard_normal((V, E)) * 1.5 / np.sqrt(V), FMT)
    return {"x": x,
            "wg_words": wg_words,
            "wg_scales": wg_scales,
            "ret": ret,
            "wo_words": wo_words,
            "wo_scales": wo_scales}


def reference(x, wg_words, wg_scales, ret, wo_words, wo_scales):
    g = mxq(f64(x), 2, "e4m3") @ unpack_weight(wg_words, wg_scales, FMT)
    r = f64(ret)
    n = r * (1.0 / np.sqrt(np.mean(r * r, axis=-1, keepdims=True) + EPS))
    h = silu(g) * n.reshape(B, S, V)
    return mxq(h, 2, "e4m3") @ unpack_weight(wo_words, wo_scales, FMT)

@@ -1,0 +1,283 @@
+from contextlib import ExitStack
+
+import concourse.mybir as mybir
+from concourse.masks import make_identity
+
+F32 = mybir.dt.float32
+BF16 = mybir.dt.bfloat16
+I32 = mybir.dt.int32
+U32 = mybir.dt.uint32
+U8 = mybir.dt.uint8
+FP8X4 = mybir.dt.float8_e4m3fn_x4
+ACT = mybir.ActivationFunctionType
+ALU = mybir.AluOpType
+
+P = 128
+PACK = 4
+K_PASS = P * PACK
+N_PASS = 512
+
+TOKENS = 256
+TOKEN_TILES = TOKENS // P
+E = 1024
+X_PASSES = E // K_PASS
+HEADS = 8
+HEAD_DIM = 1024
+V = HEADS * HEAD_DIM
+CHUNKS_PER_HEAD = HEAD_DIM // K_PASS
+CHUNKS = V // K_PASS
+OUT_TILES = E // N_PASS
+EPS = 1e-5
+PLANES_PER_TILE = 4
+QUADRANTS = 4
+
+FLOPS = 2 * TOKENS * E * V + 2 * TOKENS * V * E
+
+
+def tile_retnet_pc_k_kernel(tc, x, wg_words, wg_scales, ret, wo_words, wo_scales, out):
+    nc = tc.nc
+
+    x_view = x[0].rearrange("(tt p) k -> p tt k", p=P)
+    ret_view = ret[0].rearrange("(tt p) h d -> p tt h d", p=P)
+    out_view = out[0].rearrange("(tt p) e -> p tt e", p=P)
+    wg_view = wg_words.rearrange("g p n t -> p g (n t)")
+    wo_view = wo_words.rearrange("g p n t -> p g (n t)")
+
+    with ExitStack() as ctx:
+        keep = ctx.enter_context(tc.tile_pool(name="keep", bufs=1))
+        weights = ctx.enter_context(tc.tile_pool(name="weights", bufs=2 * HEADS))
+        rets = ctx.enter_context(tc.tile_pool(name="rets", bufs=HEADS))
+        small = ctx.enter_context(tc.tile_pool(name="small", bufs=HEADS))
+        work = ctx.enter_context(tc.tile_pool(name="work", bufs=2))
+        ring = ctx.enter_context(tc.psum_pool(name="ring", bufs=4))
+        sums = ctx.enter_context(tc.psum_pool(name="sums", bufs=1))
+        ctx.enter_context(tc.manual_schedule())
+
+        neg_half = keep.tile([P, TOKEN_TILES], F32, name="neg_half")
+        nc.gpsimd.memset(neg_half[:], -0.5)
+        ident_f32 = keep.tile([P, P], F32, name="ident_f32")
+        make_identity(nc, ident_f32[:])
+        ident_bf16 = keep.tile([P, P], BF16, name="ident_bf16")
+        make_identity(nc, ident_bf16[:])
+
+        warm = keep.tile([P, 1], F32, name="warm")
+        nc.scalar.activation(out=warm[:], in_=neg_half[:, 0:1], func=ACT.Silu)
+
+        wg_quarter = V // PLANES_PER_TILE
+        wg_planes = keep.tile([P, X_PASSES, wg_quarter], U8, name="wg_planes", align_bytes=64)
+        wo_planes = keep.tile([P, CHUNKS // PLANES_PER_TILE, E], U8, name="wo_planes", align_bytes=64)
+        nc.vector.memset(wg_planes[:].bitcast(I32), 0)
+        nc.vector.memset(wo_planes[:].bitcast(I32), 0)
+
+        x_sb = keep.tile([P, TOKEN_TILES, E], BF16, name="x_sb")
+        nc.sync.dma_start(out=x_sb[:], in_=x_view)
+
+        for g in range(X_PASSES):
+            for q in range(QUADRANTS):
+                nc.sync.dma_start(
+                    out=wg_planes[32 * q : 32 * q + 16, g, :].bitcast(I32),
+                    in_=wg_scales[g, 4 * q : 4 * q + 4, :]
+                    .bitcast(I32)
+                    .rearrange("r (j n) -> j r n", j=PLANES_PER_TILE),
+                )
+
+        ret_tiles = []
+        wg_tiles = []
+        wo_tiles = []
+
+        def load_ret(h):
+            ret_t = rets.tile([P, TOKEN_TILES, HEAD_DIM], BF16, name="ret_t", tag="ret")
+            nc.sync.dma_start(out=ret_t[:], in_=ret_view[:, :, h, :])
+            ret_tiles.append(ret_t)
+
+        def load_wg(h):
+            wg_t = weights.tile([P, X_PASSES, HEAD_DIM], U32, name="wg_t", tag="w", align_bytes=64)
+            nc.sync.dma_start(
+                out=wg_t[:].bitcast(I32),
+                in_=wg_view[:, :, PACK * HEAD_DIM * h : PACK * HEAD_DIM * (h + 1)].bitcast(I32),
+            )
+            wg_tiles.append(wg_t)
+
+        def load_wo(h):
+            wo_t = weights.tile([P, CHUNKS_PER_HEAD, E], U32, name="wo_t", tag="w", align_bytes=64)
+            nc.sync.dma_start(
+                out=wo_t[:].bitcast(I32),
+                in_=wo_view[:, CHUNKS_PER_HEAD * h : CHUNKS_PER_HEAD * (h + 1), :].bitcast(I32),
+            )
+            wo_tiles.append(wo_t)
+
+        def load_wo_planes():
+            for s in range(CHUNKS // PLANES_PER_TILE):
+                for q in range(QUADRANTS):
+                    nc.sync.dma_start(
+                        out=wo_planes[32 * q : 32 * q + 16, s, :].bitcast(I32),
+                        in_=wo_scales[
+                            PLANES_PER_TILE * s : PLANES_PER_TILE * (s + 1), 4 * q : 4 * q + 4, :
+                        ].bitcast(I32),
+                    )
+
+        load_ret(0)
+        for h in range(HEADS):
+            load_wg(h)
+            if h + 1 < HEADS:
+                load_ret(h + 1)
+            if h == 2:
+                load_wo_planes()
+            if h >= 2:
+                load_wo(h - 2)
+        load_wo(HEADS - 2)
+        load_wo(HEADS - 1)
+
+        x_codes = keep.tile([P, X_PASSES, TOKENS], U32, name="x_codes", align_bytes=64)
+        x_planes = keep.tile([P, X_PASSES, TOKENS], U8, name="x_planes", align_bytes=64)
+        words_per_pass = K_PASS // 2
+        for g in range(X_PASSES):
+            x_ps = ring.tile([P, TOKEN_TILES, 2, P], F32, name="x_ps", tag="ring")
+            for tt in range(TOKEN_TILES):
+                x_words = x_sb[:, tt, :].bitcast(F32)
+                for u in range(2):
+                    nc.tensor.transpose(
+                        out=x_ps[:, tt, u, :],
+                        in_=x_words[:, words_per_pass * g + u : words_per_pass * (g + 1) : 2],
+                        identity=ident_f32[:],
+                    )
+            x_grouped = keep.tile([P, PACK * TOKENS], BF16, name="x_grouped%d" % g, align_bytes=64)
+            grouped_words = x_grouped[:].bitcast(F32).rearrange("p (tt s u) -> p tt s u", tt=TOKEN_TILES, u=2)
+            if g == 0:
+                nc.vector.tensor_copy(out=grouped_words, in_=x_ps[:].rearrange("p tt u s -> p tt s u"))
+            else:
+                nc.scalar.copy(out=grouped_words, in_=x_ps[:].rearrange("p tt u s -> p tt s u"))
+            nc.vector.quantize_mx(
+                out=x_codes[:, g, :].bitcast(FP8X4), scales=x_planes[:, g, :], in_=x_grouped[:]
+            )
+
+        rs_tiles = []
+        h_sorted = {}
+        grouped_tiles = {}
+        h_code_tiles = {}
+        h_plane_tiles = {}
+        acc = {}
+
+        def norm_scale(h):
+            mean_sq = small.tile([P, TOKEN_TILES], F32, name="mean_sq", tag="mean_sq")
+            for tt in range(TOKEN_TILES):
+                squares = work.tile([P, HEAD_DIM], BF16, name="squares", tag="squares")
+                nc.scalar.activation(
+                    out=squares[:],
+                    in_=ret_tiles[h][:, tt, :],
+                    func=ACT.Square,
+                    scale=HEAD_DIM**-0.5,
+                    accum_out=mean_sq[:, tt : tt + 1],
+                )
+            shifted = small.tile([P, TOKEN_TILES], F32, name="shifted", tag="shifted")
+            nc.gpsimd.tensor_scalar(
+                out=shifted[:], in0=mean_sq[:], scalar1=1.0, scalar2=EPS, op0=ALU.mult, op1=ALU.add
+            )
+            rs = small.tile([P, TOKEN_TILES], F32, name="rs", tag="rs")
+            nc.gpsimd.tensor_tensor(out=rs[:], in0=shifted[:], in1=neg_half[:], op=ALU.pow)
+            rs_tiles.append(rs)
+
+        def gate(h):
+            for c in range(CHUNKS_PER_HEAD):
+                chunk = CHUNKS_PER_HEAD * h + c
+                plane = (chunk * K_PASS) // wg_quarter
+                first = (chunk * K_PASS) % wg_quarter
+                cols = slice(K_PASS * c, K_PASS * (c + 1))
+                for tt in range(TOKEN_TILES):
+                    toks = slice(P * tt, P * (tt + 1))
+                    g_ps = ring.tile([P, N_PASS], F32, name="g_ps", tag="ring")
+                    for g in range(X_PASSES):
+                        nc.tensor.matmul_mx(
+                            out=g_ps[:],
+                            lhsT=x_codes[:, g, toks].bitcast(FP8X4),
+                            lhsT_scale=x_planes[:, g, toks],
+                            rhs=wg_tiles[h][:, g, cols].bitcast(FP8X4),
+                            rhs_scale=wg_planes[4 * plane : P, g, first : first + N_PASS],
+                            start=(g == 0),
+                            stop=(g == X_PASSES - 1),
+                        )
+                    silu = work.tile([P, PACK, P], F32, name="silu", tag="silu", bufs=4)
+                    nc.scalar.activation(
+                        out=silu[:], in_=g_ps[:].rearrange("s (p t) -> s t p", t=PACK), func=ACT.Silu
+                    )
+                    hs = work.tile([P, PACK, P], BF16, name="hs", tag="hs", bufs=8)
+                    nc.vector.scalar_tensor_tensor(
+                        out=hs[:],
+                        in0=silu[:],
+                        scalar=rs_tiles[h][:, tt : tt + 1],
+                        in1=ret_tiles[h][:, tt, cols].rearrange("s (p t) -> s t p", t=PACK),
+                        op0=ALU.mult,
+                        op1=ALU.mult,
+                    )
+                    h_sorted[(h, c, tt)] = hs
+
+        def turn(h):
+            grouped = work.tile([P, CHUNKS_PER_HEAD, TOKENS, PACK], BF16, name="grouped", tag="grouped", align_bytes=64)
+            for c in range(CHUNKS_PER_HEAD):
+                t_ps = ring.tile([P, TOKEN_TILES, PACK, P], BF16, name="t_ps", tag="ring")
+                for tt in range(TOKEN_TILES):
+                    for t in range(PACK):
+                        nc.tensor.transpose(
+                            out=t_ps[:, tt, t, :], in_=h_sorted[(h, c, tt)][:, t, :], identity=ident_bf16[:]
+                        )
+                nc.vector.tensor_copy(
+                    out=grouped[:, c].rearrange("p (tt s) t -> p tt s t", tt=TOKEN_TILES),
+                    in_=t_ps[:].rearrange("p tt t s -> p tt s t"),
+                )
+            grouped_tiles[h] = grouped
+
+        def quantise(h):
+            codes = work.tile([P, CHUNKS_PER_HEAD * TOKENS], U32, name="codes", tag="codes", bufs=3, align_bytes=64)
+            planes = work.tile([P, CHUNKS_PER_HEAD * TOKENS], U8, name="planes", tag="planes", bufs=3, align_bytes=64)
+            nc.vector.quantize_mx(
+                out=codes[:].bitcast(FP8X4),
+                scales=planes[:],
+                in_=grouped_tiles[h][:].rearrange("p c s t -> p (c s t)"),
+            )
+            h_code_tiles[h] = codes
+            h_plane_tiles[h] = planes
+
+        def project(h):
+            for c in range(CHUNKS_PER_HEAD):
+                chunk = CHUNKS_PER_HEAD * h + c
+                for tt in range(TOKEN_TILES):
+                    toks = slice(TOKENS * c + P * tt, TOKENS * c + P * (tt + 1))
+                    for et in range(OUT_TILES):
+                        cols = slice(N_PASS * et, N_PASS * (et + 1))
+                        nc.tensor.matmul_mx(
+                            out=acc[(tt, et)][:],
+                            lhsT=h_code_tiles[h][:, toks].bitcast(FP8X4),
+                            lhsT_scale=h_plane_tiles[h][:, toks],
+                            rhs=wo_tiles[h][:, c, cols].bitcast(FP8X4),
+                            rhs_scale=wo_planes[
+                                4 * (chunk % PLANES_PER_TILE) : P, chunk // PLANES_PER_TILE, cols
+                            ],
+                            start=(chunk == 0),
+                            stop=(chunk == CHUNKS - 1),
+                        )
+
+        for tt in range(TOKEN_TILES):
+            for et in range(OUT_TILES):
+                acc[(tt, et)] = sums.tile([P, N_PASS], F32, name="acc%d%d" % (tt, et))
+
+        norm_scale(0)
+        for i in range(HEADS + 2):
+            if 1 <= i <= HEADS:
+                turn(i - 1)
+            if i < HEADS:
+                gate(i)
+            if 1 <= i <= HEADS:
+                quantise(i - 1)
+            if i >= 2:
+                project(i - 2)
+            if i + 1 < HEADS:
+                norm_scale(i + 1)
+
+        for tt in range(TOKEN_TILES):
+            for et in range(OUT_TILES):
+                result = work.tile([P, N_PASS], F32, name="result", tag="result", bufs=4)
+                if et == 0:
+                    nc.vector.tensor_copy(out=result[:], in_=acc[(tt, et)][:])
+                else:
+                    nc.scalar.copy(out=result[:], in_=acc[(tt, et)][:])
+                nc.sync.dma_start(out=out_view[:, tt, N_PASS * et : N_PASS * (et + 1)], in_=result[:])

@@ -196,16 +196,14 @@ def tile_retnet_pc_k_kernel(tc, x, wg_words, wg_scales, ret, wo_words, wo_scales
                             start=(g == 0),
                             stop=(g == X_PASSES - 1),
                         )
-                    silu = work.tile([P, PACK, P], F32, name="silu", tag="silu", bufs=4)
-                    nc.scalar.activation(
-                        out=silu[:], in_=g_ps[:].rearrange("s (p t) -> s t p", t=PACK), func=ACT.Silu
-                    )
+                    silu = work.tile([P, N_PASS], F32, name="silu", tag="silu", bufs=4)
+                    nc.scalar.activation(out=silu[:], in_=g_ps[:], func=ACT.Silu)
                     hs = work.tile([P, PACK, P], BF16, name="hs", tag="hs", bufs=8)
                     nc.vector.scalar_tensor_tensor(
-                        out=hs[:],
-                        in0=silu[:],
+                        out=hs[:].rearrange("s t p -> s p t"),
+                        in0=silu[:].rearrange("s (p t) -> s p t", t=PACK),
                         scalar=rs_tiles[h][:, tt : tt + 1],
-                        in1=ret_tiles[h][:, tt, cols].rearrange("s (p t) -> s t p", t=PACK),
+                        in1=ret_tiles[h][:, tt, cols].rearrange("s (p t) -> s p t", t=PACK),
                         op0=ALU.mult,
                         op1=ALU.mult,
                     )

@@ -72,14 +72,15 @@ def tile_retnet_pc_k_kernel(tc, x, wg_words, wg_scales, ret, wo_words, wo_scales
         x_sb = keep.tile([P, TOKEN_TILES, E], BF16, name="x_sb")
         nc.sync.dma_start(out=x_sb[:], in_=x_view)
 
-        for g in range(X_PASSES):
-            for q in range(QUADRANTS):
-                nc.sync.dma_start(
-                    out=wg_planes[32 * q : 32 * q + 16, g, :].bitcast(I32),
-                    in_=wg_scales[g, 4 * q : 4 * q + 4, :]
-                    .bitcast(I32)
-                    .rearrange("r (j n) -> j r n", j=PLANES_PER_TILE),
-                )
+        def load_wg_planes():
+            for g in range(X_PASSES):
+                for q in range(QUADRANTS):
+                    nc.sync.dma_start(
+                        out=wg_planes[32 * q : 32 * q + 16, g, :].bitcast(I32),
+                        in_=wg_scales[g, 4 * q : 4 * q + 4, :]
+                        .bitcast(I32)
+                        .rearrange("r (j n) -> j r n", j=PLANES_PER_TILE),
+                    )
 
         ret_tiles = []
         wg_tiles = []
@@ -90,12 +91,15 @@ def tile_retnet_pc_k_kernel(tc, x, wg_words, wg_scales, ret, wo_words, wo_scales
             nc.sync.dma_start(out=ret_t[:], in_=ret_view[:, :, h, :])
             ret_tiles.append(ret_t)
 
-        def load_wg(h):
+        def load_wg(h, pieces):
             wg_t = weights.tile([P, X_PASSES, HEAD_DIM], U32, name="wg_t", tag="w", align_bytes=64)
-            nc.sync.dma_start(
-                out=wg_t[:].bitcast(I32),
-                in_=wg_view[:, :, PACK * HEAD_DIM * h : PACK * HEAD_DIM * (h + 1)].bitcast(I32),
-            )
+            width = HEAD_DIM // pieces
+            for piece in range(pieces):
+                first = HEAD_DIM * h + width * piece
+                nc.sync.dma_start(
+                    out=wg_t[:, :, width * piece : width * (piece + 1)].bitcast(I32),
+                    in_=wg_view[:, :, PACK * first : PACK * (first + width)].bitcast(I32),
+                )
             wg_tiles.append(wg_t)
 
         def load_wo(h):
@@ -106,23 +110,21 @@ def tile_retnet_pc_k_kernel(tc, x, wg_words, wg_scales, ret, wo_words, wo_scales
             )
             wo_tiles.append(wo_t)
 
-        def load_wo_planes():
-            for s in range(CHUNKS // PLANES_PER_TILE):
-                for q in range(QUADRANTS):
-                    nc.sync.dma_start(
-                        out=wo_planes[32 * q : 32 * q + 16, s, :].bitcast(I32),
-                        in_=wo_scales[
-                            PLANES_PER_TILE * s : PLANES_PER_TILE * (s + 1), 4 * q : 4 * q + 4, :
-                        ].bitcast(I32),
-                    )
+        def load_wo_planes(s):
+            for q in range(QUADRANTS):
+                nc.gpsimd.dma_start(
+                    out=wo_planes[32 * q : 32 * q + 16, s, :].bitcast(F32),
+                    in_=wo_scales[
+                        PLANES_PER_TILE * s : PLANES_PER_TILE * (s + 1), 4 * q : 4 * q + 4, :
+                    ].bitcast(F32),
+                )
 
         load_ret(0)
+        load_wg_planes()
         for h in range(HEADS):
-            load_wg(h)
+            load_wg(h, CHUNKS_PER_HEAD if h == 0 else 1)
             if h + 1 < HEADS:
                 load_ret(h + 1)
-            if h == 2:
-                load_wo_planes()
             if h >= 2:
                 load_wo(h - 2)
         load_wo(HEADS - 2)
@@ -130,6 +132,7 @@ def tile_retnet_pc_k_kernel(tc, x, wg_words, wg_scales, ret, wo_words, wo_scales
 
         x_codes = keep.tile([P, X_PASSES, TOKENS], U32, name="x_codes", align_bytes=64)
         x_planes = keep.tile([P, X_PASSES, TOKENS], U8, name="x_planes", align_bytes=64)
+        x_grouped = keep.tile([P, X_PASSES, PACK * TOKENS], BF16, name="x_grouped", align_bytes=64)
         words_per_pass = K_PASS // 2
         for g in range(X_PASSES):
             x_ps = ring.tile([P, TOKEN_TILES, 2, P], F32, name="x_ps", tag="ring")
@@ -141,14 +144,13 @@ def tile_retnet_pc_k_kernel(tc, x, wg_words, wg_scales, ret, wo_words, wo_scales
                         in_=x_words[:, words_per_pass * g + u : words_per_pass * (g + 1) : 2],
                         identity=ident_f32[:],
                     )
-            x_grouped = keep.tile([P, PACK * TOKENS], BF16, name="x_grouped%d" % g, align_bytes=64)
-            grouped_words = x_grouped[:].bitcast(F32).rearrange("p (tt s u) -> p tt s u", tt=TOKEN_TILES, u=2)
-            if g == 0:
-                nc.vector.tensor_copy(out=grouped_words, in_=x_ps[:].rearrange("p tt u s -> p tt s u"))
-            else:
-                nc.scalar.copy(out=grouped_words, in_=x_ps[:].rearrange("p tt u s -> p tt s u"))
+            nc.vector.tensor_copy(
+                out=x_grouped[:, g, :].bitcast(F32).rearrange("p (tt s u) -> p tt s u", tt=TOKEN_TILES, u=2),
+                in_=x_ps[:].rearrange("p tt u s -> p tt s u"),
+            )
+        for g in range(X_PASSES):
             nc.vector.quantize_mx(
-                out=x_codes[:, g, :].bitcast(FP8X4), scales=x_planes[:, g, :], in_=x_grouped[:]
+                out=x_codes[:, g, :].bitcast(FP8X4), scales=x_planes[:, g, :], in_=x_grouped[:, g, :]
             )
 
         rs_tiles = []
@@ -176,6 +178,8 @@ def tile_retnet_pc_k_kernel(tc, x, wg_words, wg_scales, ret, wo_words, wo_scales
             rs = small.tile([P, TOKEN_TILES], F32, name="rs", tag="rs")
             nc.gpsimd.tensor_tensor(out=rs[:], in0=shifted[:], in1=neg_half[:], op=ALU.pow)
             rs_tiles.append(rs)
+            if h < CHUNKS // PLANES_PER_TILE:
+                load_wo_planes(h)
 
         def gate(h):
             for c in range(CHUNKS_PER_HEAD):
@@ -218,10 +222,11 @@ def tile_retnet_pc_k_kernel(tc, x, wg_words, wg_scales, ret, wo_words, wo_scales
                         nc.tensor.transpose(
                             out=t_ps[:, tt, t, :], in_=h_sorted[(h, c, tt)][:, t, :], identity=ident_bf16[:]
                         )
-                nc.vector.tensor_copy(
-                    out=grouped[:, c].rearrange("p (tt s) t -> p tt s t", tt=TOKEN_TILES),
-                    in_=t_ps[:].rearrange("p tt t s -> p tt s t"),
-                )
+                side_by_side = grouped[:, c].rearrange("p (tt s) t -> p tt s t", tt=TOKEN_TILES)
+                if (CHUNKS_PER_HEAD * h + c) % 4 == 3:
+                    nc.scalar.copy(out=side_by_side, in_=t_ps[:].rearrange("p tt t s -> p tt s t"))
+                else:
+                    nc.vector.tensor_copy(out=side_by_side, in_=t_ps[:].rearrange("p tt t s -> p tt s t"))
             grouped_tiles[h] = grouped
 
         def quantise(h):

@@ -57,8 +57,6 @@ def tile_retnet_pc_k_kernel(tc, x, wg_words, wg_scales, ret, wo_words, wo_scales
         nc.gpsimd.memset(neg_half[:], -0.5)
         ident_f32 = keep.tile([P, P], F32, name="ident_f32")
         make_identity(nc, ident_f32[:])
-        ident_bf16 = keep.tile([P, P], BF16, name="ident_bf16")
-        make_identity(nc, ident_bf16[:])
 
         warm = keep.tile([P, 1], F32, name="warm")
         nc.scalar.activation(out=warm[:], in_=neg_half[:, 0:1], func=ACT.Silu)
@@ -202,31 +200,36 @@ def tile_retnet_pc_k_kernel(tc, x, wg_words, wg_scales, ret, wo_words, wo_scales
                         )
                     silu = work.tile([P, N_PASS], F32, name="silu", tag="silu", bufs=4)
                     nc.scalar.activation(out=silu[:], in_=g_ps[:], func=ACT.Silu)
-                    hs = work.tile([P, PACK, P], BF16, name="hs", tag="hs", bufs=8)
-                    nc.vector.scalar_tensor_tensor(
-                        out=hs[:].rearrange("s t p -> s p t"),
-                        in0=silu[:].rearrange("s (p t) -> s p t", t=PACK),
-                        scalar=rs_tiles[h][:, tt : tt + 1],
-                        in1=ret_tiles[h][:, tt, cols].rearrange("s (p t) -> s p t", t=PACK),
-                        op0=ALU.mult,
-                        op1=ALU.mult,
-                    )
+                    hs = work.tile([P, 2, P, 2], BF16, name="hs", tag="hs", bufs=8)
+                    for u in range(2):
+                        nc.vector.scalar_tensor_tensor(
+                            out=hs[:, u],
+                            in0=silu[:].rearrange("s (p u e) -> s p u e", u=2, e=2)[:, :, u, :],
+                            scalar=rs_tiles[h][:, tt : tt + 1],
+                            in1=ret_tiles[h][:, tt, cols].rearrange("s (p u e) -> s p u e", u=2, e=2)[:, :, u, :],
+                            op0=ALU.mult,
+                            op1=ALU.mult,
+                        )
                     h_sorted[(h, c, tt)] = hs
 
         def turn(h):
             grouped = work.tile([P, CHUNKS_PER_HEAD, TOKENS, PACK], BF16, name="grouped", tag="grouped", align_bytes=64)
             for c in range(CHUNKS_PER_HEAD):
-                t_ps = ring.tile([P, TOKEN_TILES, PACK, P], BF16, name="t_ps", tag="ring")
+                t_ps = ring.tile([P, TOKEN_TILES, 2, P], F32, name="t_ps", tag="ring")
                 for tt in range(TOKEN_TILES):
-                    for t in range(PACK):
+                    for u in range(2):
                         nc.tensor.transpose(
-                            out=t_ps[:, tt, t, :], in_=h_sorted[(h, c, tt)][:, t, :], identity=ident_bf16[:]
+                            out=t_ps[:, tt, u, :],
+                            in_=h_sorted[(h, c, tt)][:, u].rearrange("s p e -> s (p e)").bitcast(F32),
+                            identity=ident_f32[:],
                         )
-                side_by_side = grouped[:, c].rearrange("p (tt s) t -> p tt s t", tt=TOKEN_TILES)
-                if (CHUNKS_PER_HEAD * h + c) % 4 == 3:
-                    nc.scalar.copy(out=side_by_side, in_=t_ps[:].rearrange("p tt t s -> p tt s t"))
-                else:
-                    nc.vector.tensor_copy(out=side_by_side, in_=t_ps[:].rearrange("p tt t s -> p tt s t"))
+                nc.vector.tensor_copy(
+                    out=grouped[:, c]
+                    .rearrange("p s t -> p (s t)")
+                    .bitcast(F32)
+                    .rearrange("p (tt s u) -> p tt s u", tt=TOKEN_TILES, u=2),
+                    in_=t_ps[:].rearrange("p tt u s -> p tt s u"),
+                )
             grouped_tiles[h] = grouped
 
         def quantise(h):

@@ -68,17 +68,15 @@ def tile_retnet_pc_k_kernel(tc, x, wg_words, wg_scales, ret, wo_words, wo_scales
         nc.vector.memset(wo_planes[:].bitcast(I32), 0)
 
         x_sb = keep.tile([P, TOKEN_TILES, E], BF16, name="x_sb")
-        nc.sync.dma_start(out=x_sb[:], in_=x_view)
 
-        def load_wg_planes():
-            for g in range(X_PASSES):
-                for q in range(QUADRANTS):
-                    nc.sync.dma_start(
-                        out=wg_planes[32 * q : 32 * q + 16, g, :].bitcast(I32),
-                        in_=wg_scales[g, 4 * q : 4 * q + 4, :]
-                        .bitcast(I32)
-                        .rearrange("r (j n) -> j r n", j=PLANES_PER_TILE),
-                    )
+        def load_wg_planes(g):
+            for q in range(QUADRANTS):
+                nc.sync.dma_start(
+                    out=wg_planes[32 * q : 32 * q + 16, g, :].bitcast(I32),
+                    in_=wg_scales[g, 4 * q : 4 * q + 4, :]
+                    .bitcast(I32)
+                    .rearrange("r (j n) -> j r n", j=PLANES_PER_TILE),
+                )
 
         ret_tiles = []
         wg_tiles = []
@@ -89,16 +87,15 @@ def tile_retnet_pc_k_kernel(tc, x, wg_words, wg_scales, ret, wo_words, wo_scales
             nc.sync.dma_start(out=ret_t[:], in_=ret_view[:, :, h, :])
             ret_tiles.append(ret_t)
 
-        def load_wg(h, pieces):
-            wg_t = weights.tile([P, X_PASSES, HEAD_DIM], U32, name="wg_t", tag="w", align_bytes=64)
-            width = HEAD_DIM // pieces
-            for piece in range(pieces):
-                first = HEAD_DIM * h + width * piece
-                nc.sync.dma_start(
-                    out=wg_t[:, :, width * piece : width * (piece + 1)].bitcast(I32),
-                    in_=wg_view[:, :, PACK * first : PACK * (first + width)].bitcast(I32),
-                )
-            wg_tiles.append(wg_t)
+        def load_wg(h, first_col, width):
+            if first_col == 0:
+                wg_t = weights.tile([P, X_PASSES, HEAD_DIM], U32, name="wg_t", tag="w", align_bytes=64)
+                wg_tiles.append(wg_t)
+            first = HEAD_DIM * h + first_col
+            nc.sync.dma_start(
+                out=wg_tiles[h][:, :, first_col : first_col + width].bitcast(I32),
+                in_=wg_view[:, :, PACK * first : PACK * (first + width)].bitcast(I32),
+            )
 
         def load_wo(h):
             wo_t = weights.tile([P, CHUNKS_PER_HEAD, E], U32, name="wo_t", tag="w", align_bytes=64)
@@ -118,9 +115,14 @@ def tile_retnet_pc_k_kernel(tc, x, wg_words, wg_scales, ret, wo_words, wo_scales
                 )
 
         load_ret(0)
-        load_wg_planes()
-        for h in range(HEADS):
-            load_wg(h, CHUNKS_PER_HEAD if h == 0 else 1)
+        nc.sync.dma_start(out=x_sb[:], in_=x_view)
+        load_wg_planes(0)
+        load_wg(0, 0, K_PASS)
+        load_wg_planes(1)
+        load_wg(0, K_PASS, K_PASS)
+        load_ret(1)
+        for h in range(1, HEADS):
+            load_wg(h, 0, HEAD_DIM)
             if h + 1 < HEADS:
                 load_ret(h + 1)
             if h >= 2:
@@ -244,23 +246,22 @@ def tile_retnet_pc_k_kernel(tc, x, wg_words, wg_scales, ret, wo_words, wo_scales
             h_plane_tiles[h] = planes
 
         def project(h):
-            for c in range(CHUNKS_PER_HEAD):
+            passes = [(c, tt, et) for c in range(CHUNKS_PER_HEAD) for tt in range(TOKEN_TILES) for et in range(OUT_TILES)]
+            if h == HEADS - 1:
+                passes = sorted(passes, key=lambda cte: (cte[1], cte[2], cte[0]))
+            for c, tt, et in passes:
                 chunk = CHUNKS_PER_HEAD * h + c
-                for tt in range(TOKEN_TILES):
-                    toks = slice(TOKENS * c + P * tt, TOKENS * c + P * (tt + 1))
-                    for et in range(OUT_TILES):
-                        cols = slice(N_PASS * et, N_PASS * (et + 1))
-                        nc.tensor.matmul_mx(
-                            out=acc[(tt, et)][:],
-                            lhsT=h_code_tiles[h][:, toks].bitcast(FP8X4),
-                            lhsT_scale=h_plane_tiles[h][:, toks],
-                            rhs=wo_tiles[h][:, c, cols].bitcast(FP8X4),
-                            rhs_scale=wo_planes[
-                                4 * (chunk % PLANES_PER_TILE) : P, chunk // PLANES_PER_TILE, cols
-                            ],
-                            start=(chunk == 0),
-                            stop=(chunk == CHUNKS - 1),
-                        )
+                toks = slice(TOKENS * c + P * tt, TOKENS * c + P * (tt + 1))
+                cols = slice(N_PASS * et, N_PASS * (et + 1))
+                nc.tensor.matmul_mx(
+                    out=acc[(tt, et)][:],
+                    lhsT=h_code_tiles[h][:, toks].bitcast(FP8X4),
+                    lhsT_scale=h_plane_tiles[h][:, toks],
+                    rhs=wo_tiles[h][:, c, cols].bitcast(FP8X4),
+                    rhs_scale=wo_planes[4 * (chunk % PLANES_PER_TILE) : P, chunk // PLANES_PER_TILE, cols],
+                    start=(chunk == 0),
+                    stop=(chunk == CHUNKS - 1),
+                )
 
         for tt in range(TOKEN_TILES):
             for et in range(OUT_TILES):

@@ -164,13 +164,24 @@ def tile_retnet_pc_k_kernel(tc, x, wg_words, wg_scales, ret, wo_words, wo_scales
             mean_sq = small.tile([P, TOKEN_TILES], F32, name="mean_sq", tag="mean_sq")
             for tt in range(TOKEN_TILES):
                 squares = work.tile([P, HEAD_DIM], BF16, name="squares", tag="squares")
-                nc.scalar.activation(
-                    out=squares[:],
-                    in_=ret_tiles[h][:, tt, :],
-                    func=ACT.Square,
-                    scale=HEAD_DIM**-0.5,
-                    accum_out=mean_sq[:, tt : tt + 1],
-                )
+                if tt == 1 and h % 2 == 1:
+                    nc.vector.scalar_tensor_tensor(
+                        out=squares[:],
+                        in0=ret_tiles[h][:, tt, :],
+                        scalar=1.0 / HEAD_DIM,
+                        in1=ret_tiles[h][:, tt, :],
+                        op0=ALU.mult,
+                        op1=ALU.mult,
+                        accum_out=mean_sq[:, tt : tt + 1],
+                    )
+                else:
+                    nc.scalar.activation(
+                        out=squares[:],
+                        in_=ret_tiles[h][:, tt, :],
+                        func=ACT.Square,
+                        scale=HEAD_DIM**-0.5,
+                        accum_out=mean_sq[:, tt : tt + 1],
+                    )
             shifted = small.tile([P, TOKEN_TILES], F32, name="shifted", tag="shifted")
             nc.gpsimd.tensor_scalar(
                 out=shifted[:], in0=mean_sq[:], scalar1=1.0, scalar2=EPS, op0=ALU.mult, op1=ALU.add

@@ -123,10 +123,10 @@ def tile_retnet_pc_k_kernel(tc, x, wg_words, wg_scales, ret, wo_words, wo_scales
         load_ret(1)
         for h in range(1, HEADS):
             load_wg(h, 0, HEAD_DIM)
-            if h + 1 < HEADS:
-                load_ret(h + 1)
             if h >= 2:
                 load_wo(h - 2)
+            if h + 1 < HEADS:
+                load_ret(h + 1)
         load_wo(HEADS - 2)
         load_wo(HEADS - 1)
 

@@ -97,12 +97,16 @@ def tile_retnet_pc_k_kernel(tc, x, wg_words, wg_scales, ret, wo_words, wo_scales
                 in_=wg_view[:, :, PACK * first : PACK * (first + width)].bitcast(I32),
             )
 
-        def load_wo(h):
+        def load_wo(h, pieces=1):
             wo_t = weights.tile([P, CHUNKS_PER_HEAD, E], U32, name="wo_t", tag="w", align_bytes=64)
-            nc.sync.dma_start(
-                out=wo_t[:].bitcast(I32),
-                in_=wo_view[:, CHUNKS_PER_HEAD * h : CHUNKS_PER_HEAD * (h + 1), :].bitcast(I32),
-            )
+            width = E // pieces
+            for first in range(0, E, width):
+                nc.sync.dma_start(
+                    out=wo_t[:, :, first : first + width].bitcast(I32),
+                    in_=wo_view[
+                        :, CHUNKS_PER_HEAD * h : CHUNKS_PER_HEAD * (h + 1), PACK * first : PACK * (first + width)
+                    ].bitcast(I32),
+                )
             wo_tiles.append(wo_t)
 
         def load_wo_planes(s):
@@ -128,7 +132,7 @@ def tile_retnet_pc_k_kernel(tc, x, wg_words, wg_scales, ret, wo_words, wo_scales
             if h + 1 < HEADS:
                 load_ret(h + 1)
         load_wo(HEADS - 2)
-        load_wo(HEADS - 1)
+        load_wo(HEADS - 1, OUT_TILES)
 
         x_codes = keep.tile([P, X_PASSES, TOKENS], U32, name="x_codes", align_bytes=64)
         x_planes = keep.tile([P, X_PASSES, TOKENS], U8, name="x_planes", align_bytes=64)
@@ -259,7 +263,7 @@ def tile_retnet_pc_k_kernel(tc, x, wg_words, wg_scales, ret, wo_words, wo_scales
         def project(h):
             passes = [(c, tt, et) for c in range(CHUNKS_PER_HEAD) for tt in range(TOKEN_TILES) for et in range(OUT_TILES)]
             if h == HEADS - 1:
-                passes = sorted(passes, key=lambda cte: (cte[1], cte[2], cte[0]))
+                passes = sorted(passes, key=lambda cte: (cte[2], cte[1], cte[0]))
             for c, tt, et in passes:
                 chunk = CHUNKS_PER_HEAD * h + c
                 toks = slice(TOKENS * c + P * tt, TOKENS * c + P * (tt + 1))
@@ -291,10 +295,10 @@ def tile_retnet_pc_k_kernel(tc, x, wg_words, wg_scales, ret, wo_words, wo_scales
             if i + 1 < HEADS:
                 norm_scale(i + 1)
 
-        for tt in range(TOKEN_TILES):
-            for et in range(OUT_TILES):
+        for et in range(OUT_TILES):
+            for tt in range(TOKEN_TILES):
                 result = work.tile([P, N_PASS], F32, name="result", tag="result", bufs=4)
-                if et == 0:
+                if tt == 0:
                     nc.vector.tensor_copy(out=result[:], in_=acc[(tt, et)][:])
                 else:
                     nc.scalar.copy(out=result[:], in_=acc[(tt, et)][:])

from contextlib import ExitStack

import concourse.mybir as mybir
from concourse.masks import make_identity

F32 = mybir.dt.float32
BF16 = mybir.dt.bfloat16
I32 = mybir.dt.int32
U32 = mybir.dt.uint32
U8 = mybir.dt.uint8
FP8X4 = mybir.dt.float8_e4m3fn_x4
ACT = mybir.ActivationFunctionType
ALU = mybir.AluOpType

P = 128
PACK = 4
K_PASS = P * PACK
N_PASS = 512

TOKENS = 256
TOKEN_TILES = TOKENS // P
E = 1024
X_PASSES = E // K_PASS
HEADS = 8
HEAD_DIM = 1024
V = HEADS * HEAD_DIM
CHUNKS_PER_HEAD = HEAD_DIM // K_PASS
CHUNKS = V // K_PASS
OUT_TILES = E // N_PASS
EPS = 1e-5
PLANES_PER_TILE = 4
QUADRANTS = 4

FLOPS = 2 * TOKENS * E * V + 2 * TOKENS * V * E


def tile_retnet_pc_k_kernel(tc, x, wg_words, wg_scales, ret, wo_words, wo_scales, out):
    nc = tc.nc

    x_view = x[0].rearrange("(tt p) k -> p tt k", p=P)
    ret_view = ret[0].rearrange("(tt p) h d -> p tt h d", p=P)
    out_view = out[0].rearrange("(tt p) e -> p tt e", p=P)
    wg_view = wg_words.rearrange("g p n t -> p g (n t)")
    wo_view = wo_words.rearrange("g p n t -> p g (n t)")

    with ExitStack() as ctx:
        keep = ctx.enter_context(tc.tile_pool(name="keep", bufs=1))
        weights = ctx.enter_context(tc.tile_pool(name="weights", bufs=2 * HEADS))
        rets = ctx.enter_context(tc.tile_pool(name="rets", bufs=HEADS))
        small = ctx.enter_context(tc.tile_pool(name="small", bufs=HEADS))
        work = ctx.enter_context(tc.tile_pool(name="work", bufs=2))
        ring = ctx.enter_context(tc.psum_pool(name="ring", bufs=4))
        sums = ctx.enter_context(tc.psum_pool(name="sums", bufs=1))
        ctx.enter_context(tc.manual_schedule())

        neg_half = keep.tile([P, TOKEN_TILES], F32, name="neg_half")
        nc.gpsimd.memset(neg_half[:], -0.5)
        ident_f32 = keep.tile([P, P], F32, name="ident_f32")
        make_identity(nc, ident_f32[:])

        warm = keep.tile([P, 1], F32, name="warm")
        nc.scalar.activation(out=warm[:], in_=neg_half[:, 0:1], func=ACT.Silu)

        wg_quarter = V // PLANES_PER_TILE
        wg_planes = keep.tile([P, X_PASSES, wg_quarter], U8, name="wg_planes", align_bytes=64)
        wo_planes = keep.tile([P, CHUNKS // PLANES_PER_TILE, E], U8, name="wo_planes", align_bytes=64)
        nc.vector.memset(wg_planes[:].bitcast(I32), 0)
        nc.vector.memset(wo_planes[:].bitcast(I32), 0)

        x_sb = keep.tile([P, TOKEN_TILES, E], BF16, name="x_sb")

        def load_wg_planes(g):
            for q in range(QUADRANTS):
                nc.sync.dma_start(
                    out=wg_planes[32 * q : 32 * q + 16, g, :].bitcast(I32),
                    in_=wg_scales[g, 4 * q : 4 * q + 4, :]
                    .bitcast(I32)
                    .rearrange("r (j n) -> j r n", j=PLANES_PER_TILE),
                )

        ret_tiles = []
        wg_tiles = []
        wo_tiles = []

        def load_ret(h):
            ret_t = rets.tile([P, TOKEN_TILES, HEAD_DIM], BF16, name="ret_t", tag="ret")
            nc.sync.dma_start(out=ret_t[:], in_=ret_view[:, :, h, :])
            ret_tiles.append(ret_t)

        def load_wg(h, first_col, width):
            if first_col == 0:
                wg_t = weights.tile([P, X_PASSES, HEAD_DIM], U32, name="wg_t", tag="w", align_bytes=64)
                wg_tiles.append(wg_t)
            first = HEAD_DIM * h + first_col
            nc.sync.dma_start(
                out=wg_tiles[h][:, :, first_col : first_col + width].bitcast(I32),
                in_=wg_view[:, :, PACK * first : PACK * (first + width)].bitcast(I32),
            )

        def load_wo(h, pieces=1):
            wo_t = weights.tile([P, CHUNKS_PER_HEAD, E], U32, name="wo_t", tag="w", align_bytes=64)
            width = E // pieces
            for first in range(0, E, width):
                nc.sync.dma_start(
                    out=wo_t[:, :, first : first + width].bitcast(I32),
                    in_=wo_view[
                        :, CHUNKS_PER_HEAD * h : CHUNKS_PER_HEAD * (h + 1), PACK * first : PACK * (first + width)
                    ].bitcast(I32),
                )
            wo_tiles.append(wo_t)

        def load_wo_planes(s):
            for q in range(QUADRANTS):
                nc.gpsimd.dma_start(
                    out=wo_planes[32 * q : 32 * q + 16, s, :].bitcast(F32),
                    in_=wo_scales[
                        PLANES_PER_TILE * s : PLANES_PER_TILE * (s + 1), 4 * q : 4 * q + 4, :
                    ].bitcast(F32),
                )

        load_ret(0)
        nc.sync.dma_start(out=x_sb[:], in_=x_view)
        load_wg_planes(0)
        load_wg(0, 0, K_PASS)
        load_wg_planes(1)
        load_wg(0, K_PASS, K_PASS)
        load_ret(1)
        for h in range(1, HEADS):
            load_wg(h, 0, HEAD_DIM)
            if h >= 2:
                load_wo(h - 2)
            if h + 1 < HEADS:
                load_ret(h + 1)
        load_wo(HEADS - 2)
        load_wo(HEADS - 1, OUT_TILES)

        x_codes = keep.tile([P, X_PASSES, TOKENS], U32, name="x_codes", align_bytes=64)
        x_planes = keep.tile([P, X_PASSES, TOKENS], U8, name="x_planes", align_bytes=64)
        x_grouped = keep.tile([P, X_PASSES, PACK * TOKENS], BF16, name="x_grouped", align_bytes=64)
        words_per_pass = K_PASS // 2
        for g in range(X_PASSES):
            x_ps = ring.tile([P, TOKEN_TILES, 2, P], F32, name="x_ps", tag="ring")
            for tt in range(TOKEN_TILES):
                x_words = x_sb[:, tt, :].bitcast(F32)
                for u in range(2):
                    nc.tensor.transpose(
                        out=x_ps[:, tt, u, :],
                        in_=x_words[:, words_per_pass * g + u : words_per_pass * (g + 1) : 2],
                        identity=ident_f32[:],
                    )
            nc.vector.tensor_copy(
                out=x_grouped[:, g, :].bitcast(F32).rearrange("p (tt s u) -> p tt s u", tt=TOKEN_TILES, u=2),
                in_=x_ps[:].rearrange("p tt u s -> p tt s u"),
            )
        for g in range(X_PASSES):
            nc.vector.quantize_mx(
                out=x_codes[:, g, :].bitcast(FP8X4), scales=x_planes[:, g, :], in_=x_grouped[:, g, :]
            )

        rs_tiles = []
        h_sorted = {}
        grouped_tiles = {}
        h_code_tiles = {}
        h_plane_tiles = {}
        acc = {}

        def norm_scale(h):
            mean_sq = small.tile([P, TOKEN_TILES], F32, name="mean_sq", tag="mean_sq")
            for tt in range(TOKEN_TILES):
                squares = work.tile([P, HEAD_DIM], BF16, name="squares", tag="squares")
                if tt == 1 and h % 2 == 1:
                    nc.vector.scalar_tensor_tensor(
                        out=squares[:],
                        in0=ret_tiles[h][:, tt, :],
                        scalar=1.0 / HEAD_DIM,
                        in1=ret_tiles[h][:, tt, :],
                        op0=ALU.mult,
                        op1=ALU.mult,
                        accum_out=mean_sq[:, tt : tt + 1],
                    )
                else:
                    nc.scalar.activation(
                        out=squares[:],
                        in_=ret_tiles[h][:, tt, :],
                        func=ACT.Square,
                        scale=HEAD_DIM**-0.5,
                        accum_out=mean_sq[:, tt : tt + 1],
                    )
            shifted = small.tile([P, TOKEN_TILES], F32, name="shifted", tag="shifted")
            nc.gpsimd.tensor_scalar(
                out=shifted[:], in0=mean_sq[:], scalar1=1.0, scalar2=EPS, op0=ALU.mult, op1=ALU.add
            )
            rs = small.tile([P, TOKEN_TILES], F32, name="rs", tag="rs")
            nc.gpsimd.tensor_tensor(out=rs[:], in0=shifted[:], in1=neg_half[:], op=ALU.pow)
            rs_tiles.append(rs)
            if h < CHUNKS // PLANES_PER_TILE:
                load_wo_planes(h)

        def gate(h):
            for c in range(CHUNKS_PER_HEAD):
                chunk = CHUNKS_PER_HEAD * h + c
                plane = (chunk * K_PASS) // wg_quarter
                first = (chunk * K_PASS) % wg_quarter
                cols = slice(K_PASS * c, K_PASS * (c + 1))
                for tt in range(TOKEN_TILES):
                    toks = slice(P * tt, P * (tt + 1))
                    g_ps = ring.tile([P, N_PASS], F32, name="g_ps", tag="ring")
                    for g in range(X_PASSES):
                        nc.tensor.matmul_mx(
                            out=g_ps[:],
                            lhsT=x_codes[:, g, toks].bitcast(FP8X4),
                            lhsT_scale=x_planes[:, g, toks],
                            rhs=wg_tiles[h][:, g, cols].bitcast(FP8X4),
                            rhs_scale=wg_planes[4 * plane : P, g, first : first + N_PASS],
                            start=(g == 0),
                            stop=(g == X_PASSES - 1),
                        )
                    silu = work.tile([P, N_PASS], F32, name="silu", tag="silu", bufs=4)
                    nc.scalar.activation(out=silu[:], in_=g_ps[:], func=ACT.Silu)
                    hs = work.tile([P, 2, P, 2], BF16, name="hs", tag="hs", bufs=8)
                    for u in range(2):
                        nc.vector.scalar_tensor_tensor(
                            out=hs[:, u],
                            in0=silu[:].rearrange("s (p u e) -> s p u e", u=2, e=2)[:, :, u, :],
                            scalar=rs_tiles[h][:, tt : tt + 1],
                            in1=ret_tiles[h][:, tt, cols].rearrange("s (p u e) -> s p u e", u=2, e=2)[:, :, u, :],
                            op0=ALU.mult,
                            op1=ALU.mult,
                        )
                    h_sorted[(h, c, tt)] = hs

        def turn(h):
            grouped = work.tile([P, CHUNKS_PER_HEAD, TOKENS, PACK], BF16, name="grouped", tag="grouped", align_bytes=64)
            for c in range(CHUNKS_PER_HEAD):
                t_ps = ring.tile([P, TOKEN_TILES, 2, P], F32, name="t_ps", tag="ring")
                for tt in range(TOKEN_TILES):
                    for u in range(2):
                        nc.tensor.transpose(
                            out=t_ps[:, tt, u, :],
                            in_=h_sorted[(h, c, tt)][:, u].rearrange("s p e -> s (p e)").bitcast(F32),
                            identity=ident_f32[:],
                        )
                nc.vector.tensor_copy(
                    out=grouped[:, c]
                    .rearrange("p s t -> p (s t)")
                    .bitcast(F32)
                    .rearrange("p (tt s u) -> p tt s u", tt=TOKEN_TILES, u=2),
                    in_=t_ps[:].rearrange("p tt u s -> p tt s u"),
                )
            grouped_tiles[h] = grouped

        def quantise(h):
            codes = work.tile([P, CHUNKS_PER_HEAD * TOKENS], U32, name="codes", tag="codes", bufs=3, align_bytes=64)
            planes = work.tile([P, CHUNKS_PER_HEAD * TOKENS], U8, name="planes", tag="planes", bufs=3, align_bytes=64)
            nc.vector.quantize_mx(
                out=codes[:].bitcast(FP8X4),
                scales=planes[:],
                in_=grouped_tiles[h][:].rearrange("p c s t -> p (c s t)"),
            )
            h_code_tiles[h] = codes
            h_plane_tiles[h] = planes

        def project(h):
            passes = [(c, tt, et) for c in range(CHUNKS_PER_HEAD) for tt in range(TOKEN_TILES) for et in range(OUT_TILES)]
            if h == HEADS - 1:
                passes = sorted(passes, key=lambda cte: (cte[2], cte[1], cte[0]))
            for c, tt, et in passes:
                chunk = CHUNKS_PER_HEAD * h + c
                toks = slice(TOKENS * c + P * tt, TOKENS * c + P * (tt + 1))
                cols = slice(N_PASS * et, N_PASS * (et + 1))
                nc.tensor.matmul_mx(
                    out=acc[(tt, et)][:],
                    lhsT=h_code_tiles[h][:, toks].bitcast(FP8X4),
                    lhsT_scale=h_plane_tiles[h][:, toks],
                    rhs=wo_tiles[h][:, c, cols].bitcast(FP8X4),
                    rhs_scale=wo_planes[4 * (chunk % PLANES_PER_TILE) : P, chunk // PLANES_PER_TILE, cols],
                    start=(chunk == 0),
                    stop=(chunk == CHUNKS - 1),
                )

        for tt in range(TOKEN_TILES):
            for et in range(OUT_TILES):
                acc[(tt, et)] = sums.tile([P, N_PASS], F32, name="acc%d%d" % (tt, et))

        norm_scale(0)
        for i in range(HEADS + 2):
            if 1 <= i <= HEADS:
                turn(i - 1)
            if i < HEADS:
                gate(i)
            if 1 <= i <= HEADS:
                quantise(i - 1)
            if i >= 2:
                project(i - 2)
            if i + 1 < HEADS:
                norm_scale(i + 1)

        for et in range(OUT_TILES):
            for tt in range(TOKEN_TILES):
                result = work.tile([P, N_PASS], F32, name="result", tag="result", bufs=4)
                if tt == 0:
                    nc.vector.tensor_copy(out=result[:], in_=acc[(tt, et)][:])
                else:
                    nc.scalar.copy(out=result[:], in_=acc[(tt, et)][:])
                nc.sync.dma_start(out=out_view[:, tt, N_PASS * et : N_PASS * (et + 1)], in_=result[:])
